import numpy as np
import ml_dtypes


def mxq(x, axis, fmt="e4m3"):
    dtype, down = {"e4m3": (ml_dtypes.float8_e4m3fn, 7), "e5m2": (ml_dtypes.float8_e5m2, 14)}[fmt]
    v = np.moveaxis(np.asarray(x, np.float32).astype(ml_dtypes.bfloat16).astype(np.float64), axis, -1)
    blocks = v.reshape(v.shape[:-1] + (-1, 32))
    amax = np.abs(blocks).max(-1, keepdims=True)
    byte = np.maximum(np.where(amax > 0, np.frexp(amax)[1] - 1 + 127, 0) - down, 1)
    scale = np.exp2(byte - 127.0)
    codes = (blocks / scale).astype(np.float32).astype(dtype).astype(np.float64)
    return np.moveaxis((codes * scale).reshape(v.shape), -1, axis)


WIDE = False


def mx_kscale(k):
    if not WIDE:
        return np.ones(k)
    levels = np.array([10, -10, 5, -5, 0])
    a = np.random.permutation(np.resize(levels, k // 512 * 4)).reshape(k // 512, 4)
    idx = np.arange(k)
    return np.exp2(a[idx // 512, idx % 128 // 32])


BF16 = ml_dtypes.bfloat16


def bf(x):
    return np.asarray(x, np.float32).astype(BF16)


def f64(x):
    return np.asarray(x).astype(np.float64)


B, S, D, H, HD, M, G = 4, 128, 1024, 8, 128, 4096, 3
EPS = 1e-6


def rmsnorm(x, gain):
    var = np.mean(np.square(x), axis=-1, keepdims=True)
    return x * (1.0 / np.sqrt(var + EPS)) * gain


def setup_inputs():
    s = mx_kscale(D)
    return {"x": bf(np.random.standard_normal((B, S, D))),
            "rms1_scale": bf((1.0 + 0.1 * np.random.standard_normal(D)) * s),
            "w_qkv": bf(np.random.standard_normal((D, G * H * HD)) / np.sqrt(D) / s[:, None])}


def reference(x, rms1_scale, w_qkv):
    h = rmsnorm(f64(x), f64(rms1_scale))
    qkv = mxq(h, 2, "e4m3") @ mxq(f64(w_qkv), 0, "e4m3")
    qkv = qkv.reshape(B, S, G, H, HD)
    return qkv[:, :, 0], qkv[:, :, 1], qkv[:, :, 2]

@@ -1,0 +1,164 @@
+from contextlib import ExitStack
+
+import concourse.masks as masks
+import concourse.mybir as mybir
+
+BF16 = mybir.dt.bfloat16
+F32 = mybir.dt.float32
+U32 = mybir.dt.uint32
+U8 = mybir.dt.uint8
+FP8X4 = mybir.dt.float8_e4m3fn_x4
+ACT = mybir.ActivationFunctionType
+ALU = mybir.AluOpType
+
+P = 128
+PACK = 4
+K_PASS = P * PACK
+BATCH = 4
+D = 1024
+PASSES = D // K_PASS
+PROJ = 3
+PROJ_COLS = 1024
+N_TILE = 512
+HALVES = PROJ_COLS // N_TILE
+RUN = 4
+EPS = 1e-6
+
+FLOPS = 2 * BATCH * P * D * PROJ * PROJ_COLS
+
+
+def tile_transformerblocktpu_pa_kernel(tc, x, rms1_scale, w_qkv, out_0, out_1, out_2):
+    nc = tc.nc
+    outs = [o.rearrange("b s h d -> b s (h d)") for o in (out_0, out_1, out_2)]
+    w_rows = w_qkv.rearrange("(c t p) n -> c p t n", t=PACK, p=P)
+
+    with ExitStack() as ctx:
+        const = ctx.enter_context(tc.tile_pool(name="const", bufs=1))
+        keep = ctx.enter_context(tc.tile_pool(name="keep", bufs=1))
+        per_batch = ctx.enter_context(tc.tile_pool(name="per_batch", bufs=BATCH))
+        w_in = ctx.enter_context(tc.tile_pool(name="w_in", bufs=PROJ * PASSES))
+        w_stage = ctx.enter_context(tc.tile_pool(name="w_stage", bufs=2 * PASSES))
+        out_stage = ctx.enter_context(tc.tile_pool(name="out_stage", bufs=2 * BATCH))
+        psum = ctx.enter_context(tc.psum_pool(name="psum", bufs=8))
+
+        identity = const.tile([P, P], BF16)
+        masks.make_identity(nc, identity[:])
+        ones = const.tile([P, P], BF16)
+        nc.vector.memset(ones[:], 1.0)
+        eps = const.tile([P, 1], F32)
+        nc.vector.memset(eps[:], EPS)
+        gain_rows = const.tile([P, D], BF16)
+        nc.vector.memset(gain_rows[:], 0.0)
+        nc.scalar.dma_start(out=gain_rows[0:1, :], in_=rms1_scale.rearrange("(o k) -> o k", o=1))
+        warm = const.tile([P, 1], F32)
+        nc.scalar.activation(out=warm[:], in_=eps[:], func=ACT.Sqrt)
+
+        x_sb = []
+        for b in range(BATCH):
+            x_tile = per_batch.tile([P, D], BF16, name="x_tile")
+            nc.sync.dma_start(out=x_tile[:], in_=x[b])
+            x_sb.append(x_tile)
+        w_raw = {}
+        for j in range(PROJ):
+            for c in range(PASSES):
+                raw = w_in.tile([P, PACK, PROJ_COLS], BF16, name="w_raw")
+                nc.sync.dma_start(
+                    out=raw[:], in_=w_rows[c, :, :, j * PROJ_COLS : (j + 1) * PROJ_COLS]
+                )
+                w_raw[(j, c)] = raw
+
+        gain_all = const.tile([P, D], BF16)
+        for half in range(D // N_TILE):
+            cols = slice(half * N_TILE, (half + 1) * N_TILE)
+            spread = psum.tile([P, N_TILE], F32, tag="bank", name="spread")
+            nc.tensor.matmul(
+                out=spread[:], lhsT=ones[:], rhs=gain_rows[:, cols], start=True, stop=True
+            )
+            nc.vector.tensor_copy(out=gain_all[:, cols], in_=spread[:])
+
+        h_sb = []
+        for b in range(BATCH):
+            squares = per_batch.tile([P, D], BF16, name="squares")
+            mean_sq = per_batch.tile([P, 1], F32, name="mean_sq")
+            nc.scalar.activation(
+                out=squares[:],
+                in_=x_sb[b][:],
+                func=ACT.Square,
+                scale=D**-0.5,
+                accum_out=mean_sq[:],
+            )
+            rms = per_batch.tile([P, 1], F32, name="rms")
+            nc.scalar.activation(out=rms[:], in_=mean_sq[:], func=ACT.Sqrt, bias=eps[:])
+            inv_rms = per_batch.tile([P, 1], F32, name="inv_rms")
+            nc.vector.reciprocal(out=inv_rms[:], in_=rms[:])
+            h = per_batch.tile([P, D], BF16, name="h")
+            nc.vector.scalar_tensor_tensor(
+                out=h[:],
+                in0=x_sb[b][:],
+                scalar=inv_rms[:],
+                in1=gain_all[:],
+                op0=ALU.mult,
+                op1=ALU.mult,
+            )
+            h_sb.append(h)
+
+        h_grouped = keep.tile([P, BATCH, PASSES, P, PACK], BF16, align_bytes=64)
+        h_codes = keep.tile([P, BATCH, PASSES * P], U32, align_bytes=64)
+        h_scales = keep.tile([P, BATCH, PASSES * P], U8, align_bytes=64)
+        for b in range(BATCH):
+            for c in range(PASSES):
+                h_t = psum.tile([P, PACK, P], BF16, tag="bank", name="h_t")
+                for t in range(PACK):
+                    k0 = c * K_PASS + t * P
+                    nc.tensor.transpose(
+                        out=h_t[:, t, :], in_=h_sb[b][:, k0 : k0 + P], identity=identity[:]
+                    )
+                nc.scalar.copy(
+                    out=h_grouped[:, b, c, :, :], in_=h_t[:].rearrange("p t s -> p s t")
+                )
+            nc.vector.quantize_mx(
+                out=h_codes[:, b, :].bitcast(FP8X4),
+                scales=h_scales[:, b, :],
+                in_=h_grouped[:, b].rearrange("p c s t -> p (c s t)"),
+            )
+
+        w_codes = keep.tile([P, PROJ * HALVES, PASSES, N_TILE], U32, align_bytes=64)
+        w_scales = keep.tile([P, PROJ * HALVES, PASSES, N_TILE], U8, align_bytes=64)
+        for j in range(PROJ):
+            for half in range(HALVES):
+                u = j * HALVES + half
+                cols = slice(half * N_TILE, (half + 1) * N_TILE)
+
+                w_grouped = []
+                for c in range(PASSES):
+                    grouped = w_stage.tile([P, N_TILE, PACK], BF16, align_bytes=64, name="grouped")
+                    nc.vector.tensor_copy(
+                        out=grouped[:].rearrange("p (a i) t -> p a t i", i=RUN),
+                        in_=w_raw[(j, c)][:, :, cols].rearrange("p t (a i) -> p a t i", i=RUN),
+                    )
+                    w_grouped.append(grouped)
+                for c in range(PASSES):
+                    nc.vector.quantize_mx(
+                        out=w_codes[:, u, c, :].bitcast(FP8X4),
+                        scales=w_scales[:, u, c, :],
+                        in_=w_grouped[c][:].rearrange("p n t -> p (n t)"),
+                    )
+
+                accs = [
+                    psum.tile([P, N_TILE], F32, tag="bank", name="acc") for b in range(BATCH)
+                ]
+                for c in range(PASSES):
+                    for b in range(BATCH):
+                        nc.tensor.matmul_mx(
+                            out=accs[b][:],
+                            lhsT=h_codes[:, b, c * P : (c + 1) * P].bitcast(FP8X4),
+                            lhsT_scale=h_scales[:, b, c * P : (c + 1) * P],
+                            rhs=w_codes[:, u, c, :].bitcast(FP8X4),
+                            rhs_scale=w_scales[:, u, c, :],
+                            start=(c == 0),
+                            stop=(c == PASSES - 1),
+                        )
+                for b in range(BATCH):
+                    result = out_stage.tile([P, N_TILE], F32, name="result")
+                    nc.scalar.copy(out=result[:], in_=accs[b][:])
+                    nc.sync.dma_start(out=outs[j][b, :, cols], in_=result[:])

@@ -7,6 +7,7 @@ BF16 = mybir.dt.bfloat16
 F32 = mybir.dt.float32
 U32 = mybir.dt.uint32
 U8 = mybir.dt.uint8
+I32 = mybir.dt.int32
 FP8X4 = mybir.dt.float8_e4m3fn_x4
 ACT = mybir.ActivationFunctionType
 ALU = mybir.AluOpType
@@ -22,6 +23,9 @@ PROJ_COLS = 1024
 N_TILE = 512
 HALVES = PROJ_COLS // N_TILE
 RUN = 4
+SCALAR_COLS = 64
+VECTOR_RUNS = (N_TILE - SCALAR_COLS) // RUN
+UNITS = PROJ * HALVES
 EPS = 1e-6
 
 FLOPS = 2 * BATCH * P * D * PROJ * PROJ_COLS
@@ -41,15 +45,15 @@ def tile_transformerblocktpu_pa_kernel(tc, x, rms1_scale, w_qkv, out_0, out_1, o
         out_stage = ctx.enter_context(tc.tile_pool(name="out_stage", bufs=2 * BATCH))
         psum = ctx.enter_context(tc.psum_pool(name="psum", bufs=8))
 
-        identity = const.tile([P, P], BF16)
-        masks.make_identity(nc, identity[:])
+        gain_rows = const.tile([P, D], BF16)
+        nc.vector.memset(gain_rows[:].bitcast(I32), 0)
+        nc.sync.dma_start(out=gain_rows[0:1, :], in_=rms1_scale.rearrange("(o k) -> o k", o=1))
         ones = const.tile([P, P], BF16)
         nc.vector.memset(ones[:], 1.0)
         eps = const.tile([P, 1], F32)
         nc.vector.memset(eps[:], EPS)
-        gain_rows = const.tile([P, D], BF16)
-        nc.vector.memset(gain_rows[:], 0.0)
-        nc.scalar.dma_start(out=gain_rows[0:1, :], in_=rms1_scale.rearrange("(o k) -> o k", o=1))
+        identity = const.tile([P, P], BF16)
+        masks.make_identity(nc, identity[:])
         warm = const.tile([P, 1], F32)
         nc.scalar.activation(out=warm[:], in_=eps[:], func=ACT.Sqrt)
 
@@ -67,14 +71,17 @@ def tile_transformerblocktpu_pa_kernel(tc, x, rms1_scale, w_qkv, out_0, out_1, o
                 )
                 w_raw[(j, c)] = raw
 
-        gain_all = const.tile([P, D], BF16)
-        for half in range(D // N_TILE):
-            cols = slice(half * N_TILE, (half + 1) * N_TILE)
+        gain_all = []
+        for bank in range(D // N_TILE):
             spread = psum.tile([P, N_TILE], F32, tag="bank", name="spread")
             nc.tensor.matmul(
-                out=spread[:], lhsT=ones[:], rhs=gain_rows[:, cols], start=True, stop=True
+                out=spread[:],
+                lhsT=ones[:],
+                rhs=gain_rows[:, bank * N_TILE : (bank + 1) * N_TILE],
+                start=True,
+                stop=True,
             )
-            nc.vector.tensor_copy(out=gain_all[:, cols], in_=spread[:])
+            gain_all.append(spread)
 
         h_sb = []
         for b in range(BATCH):
@@ -92,14 +99,16 @@ def tile_transformerblocktpu_pa_kernel(tc, x, rms1_scale, w_qkv, out_0, out_1, o
             inv_rms = per_batch.tile([P, 1], F32, name="inv_rms")
             nc.vector.reciprocal(out=inv_rms[:], in_=rms[:])
             h = per_batch.tile([P, D], BF16, name="h")
-            nc.vector.scalar_tensor_tensor(
-                out=h[:],
-                in0=x_sb[b][:],
-                scalar=inv_rms[:],
-                in1=gain_all[:],
-                op0=ALU.mult,
-                op1=ALU.mult,
-            )
+            for bank in range(D // N_TILE):
+                feats = slice(bank * N_TILE, (bank + 1) * N_TILE)
+                nc.vector.scalar_tensor_tensor(
+                    out=h[:, feats],
+                    in0=x_sb[b][:, feats],
+                    scalar=inv_rms[:],
+                    in1=gain_all[bank][:],
+                    op0=ALU.mult,
+                    op1=ALU.mult,
+                )
             h_sb.append(h)
 
         h_grouped = keep.tile([P, BATCH, PASSES, P, PACK], BF16, align_bytes=64)
@@ -122,8 +131,8 @@ def tile_transformerblocktpu_pa_kernel(tc, x, rms1_scale, w_qkv, out_0, out_1, o
                 in_=h_grouped[:, b].rearrange("p c s t -> p (c s t)"),
             )
 
-        w_codes = keep.tile([P, PROJ * HALVES, PASSES, N_TILE], U32, align_bytes=64)
-        w_scales = keep.tile([P, PROJ * HALVES, PASSES, N_TILE], U8, align_bytes=64)
+        w_codes = keep.tile([P, UNITS, PASSES, N_TILE], U32, align_bytes=64)
+        w_scales = keep.tile([P, UNITS, PASSES, N_TILE], U8, align_bytes=64)
         for j in range(PROJ):
             for half in range(HALVES):
                 u = j * HALVES + half
@@ -132,10 +141,10 @@ def tile_transformerblocktpu_pa_kernel(tc, x, rms1_scale, w_qkv, out_0, out_1, o
                 w_grouped = []
                 for c in range(PASSES):
                     grouped = w_stage.tile([P, N_TILE, PACK], BF16, align_bytes=64, name="grouped")
-                    nc.vector.tensor_copy(
-                        out=grouped[:].rearrange("p (a i) t -> p a t i", i=RUN),
-                        in_=w_raw[(j, c)][:, :, cols].rearrange("p t (a i) -> p a t i", i=RUN),
-                    )
+                    by_column = grouped[:].rearrange("p (a i) t -> p a t i", i=RUN)
+                    by_row = w_raw[(j, c)][:, :, cols].rearrange("p t (a i) -> p a t i", i=RUN)
+                    nc.vector.tensor_copy(out=by_column[:, :VECTOR_RUNS], in_=by_row[:, :VECTOR_RUNS])
+                    nc.scalar.copy(out=by_column[:, VECTOR_RUNS:], in_=by_row[:, VECTOR_RUNS:])
                     w_grouped.append(grouped)
                 for c in range(PASSES):
                     nc.vector.quantize_mx(
@@ -160,5 +169,8 @@ def tile_transformerblocktpu_pa_kernel(tc, x, rms1_scale, w_qkv, out_0, out_1, o
                         )
                 for b in range(BATCH):
                     result = out_stage.tile([P, N_TILE], F32, name="result")
-                    nc.scalar.copy(out=result[:], in_=accs[b][:])
+                    if u == UNITS - 1 and b % 2 == 1:
+                        nc.vector.tensor_copy(out=result[:], in_=accs[b][:])
+                    else:
+                        nc.scalar.copy(out=result[:], in_=accs[b][:])
                     nc.sync.dma_start(out=outs[j][b, :, cols], in_=result[:])

@@ -26,6 +26,9 @@ RUN = 4
 SCALAR_COLS = 64
 VECTOR_RUNS = (N_TILE - SCALAR_COLS) // RUN
 UNITS = PROJ * HALVES
+W_CHUNKS = 2
+CHUNK_COLS = PROJ * PROJ_COLS // W_CHUNKS
+CHUNK_UNITS = UNITS // W_CHUNKS
 EPS = 1e-6
 
 FLOPS = 2 * BATCH * P * D * PROJ * PROJ_COLS
@@ -40,7 +43,7 @@ def tile_transformerblocktpu_pa_kernel(tc, x, rms1_scale, w_qkv, out_0, out_1, o
         const = ctx.enter_context(tc.tile_pool(name="const", bufs=1))
         keep = ctx.enter_context(tc.tile_pool(name="keep", bufs=1))
         per_batch = ctx.enter_context(tc.tile_pool(name="per_batch", bufs=BATCH))
-        w_in = ctx.enter_context(tc.tile_pool(name="w_in", bufs=PROJ * PASSES))
+        w_in = ctx.enter_context(tc.tile_pool(name="w_in", bufs=W_CHUNKS * PASSES))
         w_stage = ctx.enter_context(tc.tile_pool(name="w_stage", bufs=2 * PASSES))
         out_stage = ctx.enter_context(tc.tile_pool(name="out_stage", bufs=2 * BATCH))
         psum = ctx.enter_context(tc.psum_pool(name="psum", bufs=8))
@@ -63,13 +66,13 @@ def tile_transformerblocktpu_pa_kernel(tc, x, rms1_scale, w_qkv, out_0, out_1, o
             nc.sync.dma_start(out=x_tile[:], in_=x[b])
             x_sb.append(x_tile)
         w_raw = {}
-        for j in range(PROJ):
+        for chunk in range(W_CHUNKS):
             for c in range(PASSES):
-                raw = w_in.tile([P, PACK, PROJ_COLS], BF16, name="w_raw")
+                raw = w_in.tile([P, PACK, CHUNK_COLS], BF16, name="w_raw")
                 nc.sync.dma_start(
-                    out=raw[:], in_=w_rows[c, :, :, j * PROJ_COLS : (j + 1) * PROJ_COLS]
+                    out=raw[:], in_=w_rows[c, :, :, chunk * CHUNK_COLS : (chunk + 1) * CHUNK_COLS]
                 )
-                w_raw[(j, c)] = raw
+                w_raw[(chunk, c)] = raw
 
         gain_all = []
         for bank in range(D // N_TILE):
@@ -137,12 +140,14 @@ def tile_transformerblocktpu_pa_kernel(tc, x, rms1_scale, w_qkv, out_0, out_1, o
             for half in range(HALVES):
                 u = j * HALVES + half
                 cols = slice(half * N_TILE, (half + 1) * N_TILE)
+                chunk = u // CHUNK_UNITS
+                chunk_cols = slice((u % CHUNK_UNITS) * N_TILE, (u % CHUNK_UNITS + 1) * N_TILE)
 
                 w_grouped = []
                 for c in range(PASSES):
                     grouped = w_stage.tile([P, N_TILE, PACK], BF16, align_bytes=64, name="grouped")
                     by_column = grouped[:].rearrange("p (a i) t -> p a t i", i=RUN)
-                    by_row = w_raw[(j, c)][:, :, cols].rearrange("p t (a i) -> p a t i", i=RUN)
+                    by_row = w_raw[(chunk, c)][:, :, chunk_cols].rearrange("p t (a i) -> p a t i", i=RUN)
                     nc.vector.tensor_copy(out=by_column[:, :VECTOR_RUNS], in_=by_row[:, :VECTOR_RUNS])
                     nc.scalar.copy(out=by_column[:, VECTOR_RUNS:], in_=by_row[:, VECTOR_RUNS:])
                     w_grouped.append(grouped)

@@ -23,12 +23,10 @@ PROJ_COLS = 1024
 N_TILE = 512
 HALVES = PROJ_COLS // N_TILE
 RUN = 4
-SCALAR_COLS = 64
+SCALAR_COLS = 96
 VECTOR_RUNS = (N_TILE - SCALAR_COLS) // RUN
 UNITS = PROJ * HALVES
-W_CHUNKS = 2
-CHUNK_COLS = PROJ * PROJ_COLS // W_CHUNKS
-CHUNK_UNITS = UNITS // W_CHUNKS
+SHARED_UNITS = 2
 EPS = 1e-6
 
 FLOPS = 2 * BATCH * P * D * PROJ * PROJ_COLS
@@ -43,7 +41,7 @@ def tile_transformerblocktpu_pa_kernel(tc, x, rms1_scale, w_qkv, out_0, out_1, o
         const = ctx.enter_context(tc.tile_pool(name="const", bufs=1))
         keep = ctx.enter_context(tc.tile_pool(name="keep", bufs=1))
         per_batch = ctx.enter_context(tc.tile_pool(name="per_batch", bufs=BATCH))
-        w_in = ctx.enter_context(tc.tile_pool(name="w_in", bufs=W_CHUNKS * PASSES))
+        w_in = ctx.enter_context(tc.tile_pool(name="w_in", bufs=PROJ * PASSES))
         w_stage = ctx.enter_context(tc.tile_pool(name="w_stage", bufs=2 * PASSES))
         out_stage = ctx.enter_context(tc.tile_pool(name="out_stage", bufs=2 * BATCH))
         psum = ctx.enter_context(tc.psum_pool(name="psum", bufs=8))
@@ -66,13 +64,13 @@ def tile_transformerblocktpu_pa_kernel(tc, x, rms1_scale, w_qkv, out_0, out_1, o
             nc.sync.dma_start(out=x_tile[:], in_=x[b])
             x_sb.append(x_tile)
         w_raw = {}
-        for chunk in range(W_CHUNKS):
+        for j in range(PROJ):
             for c in range(PASSES):
-                raw = w_in.tile([P, PACK, CHUNK_COLS], BF16, name="w_raw")
+                raw = w_in.tile([P, PACK, PROJ_COLS], BF16, name="w_raw")
                 nc.sync.dma_start(
-                    out=raw[:], in_=w_rows[c, :, :, chunk * CHUNK_COLS : (chunk + 1) * CHUNK_COLS]
+                    out=raw[:], in_=w_rows[c, :, :, j * PROJ_COLS : (j + 1) * PROJ_COLS]
                 )
-                w_raw[(chunk, c)] = raw
+                w_raw[(j, c)] = raw
 
         gain_all = []
         for bank in range(D // N_TILE):
@@ -136,46 +134,50 @@ def tile_transformerblocktpu_pa_kernel(tc, x, rms1_scale, w_qkv, out_0, out_1, o
 
         w_codes = keep.tile([P, UNITS, PASSES, N_TILE], U32, align_bytes=64)
         w_scales = keep.tile([P, UNITS, PASSES, N_TILE], U8, align_bytes=64)
-        for j in range(PROJ):
-            for half in range(HALVES):
-                u = j * HALVES + half
-                cols = slice(half * N_TILE, (half + 1) * N_TILE)
-                chunk = u // CHUNK_UNITS
-                chunk_cols = slice((u % CHUNK_UNITS) * N_TILE, (u % CHUNK_UNITS + 1) * N_TILE)
 
-                w_grouped = []
-                for c in range(PASSES):
-                    grouped = w_stage.tile([P, N_TILE, PACK], BF16, align_bytes=64, name="grouped")
-                    by_column = grouped[:].rearrange("p (a i) t -> p a t i", i=RUN)
-                    by_row = w_raw[(chunk, c)][:, :, chunk_cols].rearrange("p t (a i) -> p a t i", i=RUN)
-                    nc.vector.tensor_copy(out=by_column[:, :VECTOR_RUNS], in_=by_row[:, :VECTOR_RUNS])
-                    nc.scalar.copy(out=by_column[:, VECTOR_RUNS:], in_=by_row[:, VECTOR_RUNS:])
-                    w_grouped.append(grouped)
-                for c in range(PASSES):
-                    nc.vector.quantize_mx(
-                        out=w_codes[:, u, c, :].bitcast(FP8X4),
-                        scales=w_scales[:, u, c, :],
-                        in_=w_grouped[c][:].rearrange("p n t -> p (n t)"),
-                    )
+        def prepare(u):
+            j, half = divmod(u, HALVES)
+            cols = slice(half * N_TILE, (half + 1) * N_TILE)
+            w_grouped = []
+            for c in range(PASSES):
+                grouped = w_stage.tile([P, N_TILE, PACK], BF16, align_bytes=64, name="grouped")
+                by_column = grouped[:].rearrange("p (a i) t -> p a t i", i=RUN)
+                by_row = w_raw[(j, c)][:, :, cols].rearrange("p t (a i) -> p a t i", i=RUN)
+                nc.vector.tensor_copy(out=by_column[:, :VECTOR_RUNS], in_=by_row[:, :VECTOR_RUNS])
+                nc.scalar.copy(out=by_column[:, VECTOR_RUNS:], in_=by_row[:, VECTOR_RUNS:])
+                w_grouped.append(grouped)
+            for c in range(PASSES):
+                nc.vector.quantize_mx(
+                    out=w_codes[:, u, c, :].bitcast(FP8X4),
+                    scales=w_scales[:, u, c, :],
+                    in_=w_grouped[c][:].rearrange("p n t -> p (n t)"),
+                )
 
-                accs = [
-                    psum.tile([P, N_TILE], F32, tag="bank", name="acc") for b in range(BATCH)
-                ]
-                for c in range(PASSES):
-                    for b in range(BATCH):
-                        nc.tensor.matmul_mx(
-                            out=accs[b][:],
-                            lhsT=h_codes[:, b, c * P : (c + 1) * P].bitcast(FP8X4),
-                            lhsT_scale=h_scales[:, b, c * P : (c + 1) * P],
-                            rhs=w_codes[:, u, c, :].bitcast(FP8X4),
-                            rhs_scale=w_scales[:, u, c, :],
-                            start=(c == 0),
-                            stop=(c == PASSES - 1),
-                        )
+        def project(u):
+            j, half = divmod(u, HALVES)
+            cols = slice(half * N_TILE, (half + 1) * N_TILE)
+            accs = [psum.tile([P, N_TILE], F32, tag="bank", name="acc") for b in range(BATCH)]
+            for c in range(PASSES):
                 for b in range(BATCH):
-                    result = out_stage.tile([P, N_TILE], F32, name="result")
-                    if u == UNITS - 1 and b % 2 == 1:
-                        nc.vector.tensor_copy(out=result[:], in_=accs[b][:])
-                    else:
-                        nc.scalar.copy(out=result[:], in_=accs[b][:])
-                    nc.sync.dma_start(out=outs[j][b, :, cols], in_=result[:])
+                    nc.tensor.matmul_mx(
+                        out=accs[b][:],
+                        lhsT=h_codes[:, b, c * P : (c + 1) * P].bitcast(FP8X4),
+                        lhsT_scale=h_scales[:, b, c * P : (c + 1) * P],
+                        rhs=w_codes[:, u, c, :].bitcast(FP8X4),
+                        rhs_scale=w_scales[:, u, c, :],
+                        start=(c == 0),
+                        stop=(c == PASSES - 1),
+                    )
+            for b in range(BATCH):
+                result = out_stage.tile([P, N_TILE], F32, name="result")
+                if u >= UNITS - SHARED_UNITS and b % 2 == 1:
+                    nc.vector.tensor_copy(out=result[:], in_=accs[b][:])
+                else:
+                    nc.scalar.copy(out=result[:], in_=accs[b][:])
+                nc.sync.dma_start(out=outs[j][b, :, cols], in_=result[:])
+
+        prepare(0)
+        for u in range(UNITS):
+            if u + 1 < UNITS:
+                prepare(u + 1)
+            project(u)

from contextlib import ExitStack

import concourse.masks as masks
import concourse.mybir as mybir

BF16 = mybir.dt.bfloat16
F32 = mybir.dt.float32
U32 = mybir.dt.uint32
U8 = mybir.dt.uint8
I32 = mybir.dt.int32
FP8X4 = mybir.dt.float8_e4m3fn_x4
ACT = mybir.ActivationFunctionType
ALU = mybir.AluOpType

P = 128
PACK = 4
K_PASS = P * PACK
BATCH = 4
D = 1024
PASSES = D // K_PASS
PROJ = 3
PROJ_COLS = 1024
N_TILE = 512
HALVES = PROJ_COLS // N_TILE
RUN = 4
SCALAR_COLS = 96
VECTOR_RUNS = (N_TILE - SCALAR_COLS) // RUN
UNITS = PROJ * HALVES
SHARED_UNITS = 2
EPS = 1e-6

FLOPS = 2 * BATCH * P * D * PROJ * PROJ_COLS


def tile_transformerblocktpu_pa_kernel(tc, x, rms1_scale, w_qkv, out_0, out_1, out_2):
    nc = tc.nc
    outs = [o.rearrange("b s h d -> b s (h d)") for o in (out_0, out_1, out_2)]
    w_rows = w_qkv.rearrange("(c t p) n -> c p t n", t=PACK, p=P)

    with ExitStack() as ctx:
        const = ctx.enter_context(tc.tile_pool(name="const", bufs=1))
        keep = ctx.enter_context(tc.tile_pool(name="keep", bufs=1))
        per_batch = ctx.enter_context(tc.tile_pool(name="per_batch", bufs=BATCH))
        w_in = ctx.enter_context(tc.tile_pool(name="w_in", bufs=PROJ * PASSES))
        w_stage = ctx.enter_context(tc.tile_pool(name="w_stage", bufs=2 * PASSES))
        out_stage = ctx.enter_context(tc.tile_pool(name="out_stage", bufs=2 * BATCH))
        psum = ctx.enter_context(tc.psum_pool(name="psum", bufs=8))

        gain_rows = const.tile([P, D], BF16)
        nc.vector.memset(gain_rows[:].bitcast(I32), 0)
        nc.sync.dma_start(out=gain_rows[0:1, :], in_=rms1_scale.rearrange("(o k) -> o k", o=1))
        ones = const.tile([P, P], BF16)
        nc.vector.memset(ones[:], 1.0)
        eps = const.tile([P, 1], F32)
        nc.vector.memset(eps[:], EPS)
        identity = const.tile([P, P], BF16)
        masks.make_identity(nc, identity[:])
        warm = const.tile([P, 1], F32)
        nc.scalar.activation(out=warm[:], in_=eps[:], func=ACT.Sqrt)

        x_sb = []
        for b in range(BATCH):
            x_tile = per_batch.tile([P, D], BF16, name="x_tile")
            nc.sync.dma_start(out=x_tile[:], in_=x[b])
            x_sb.append(x_tile)
        w_raw = {}
        for j in range(PROJ):
            for c in range(PASSES):
                raw = w_in.tile([P, PACK, PROJ_COLS], BF16, name="w_raw")
                nc.sync.dma_start(
                    out=raw[:], in_=w_rows[c, :, :, j * PROJ_COLS : (j + 1) * PROJ_COLS]
                )
                w_raw[(j, c)] = raw

        gain_all = []
        for bank in range(D // N_TILE):
            spread = psum.tile([P, N_TILE], F32, tag="bank", name="spread")
            nc.tensor.matmul(
                out=spread[:],
                lhsT=ones[:],
                rhs=gain_rows[:, bank * N_TILE : (bank + 1) * N_TILE],
                start=True,
                stop=True,
            )
            gain_all.append(spread)

        h_sb = []
        for b in range(BATCH):
            squares = per_batch.tile([P, D], BF16, name="squares")
            mean_sq = per_batch.tile([P, 1], F32, name="mean_sq")
            nc.scalar.activation(
                out=squares[:],
                in_=x_sb[b][:],
                func=ACT.Square,
                scale=D**-0.5,
                accum_out=mean_sq[:],
            )
            rms = per_batch.tile([P, 1], F32, name="rms")
            nc.scalar.activation(out=rms[:], in_=mean_sq[:], func=ACT.Sqrt, bias=eps[:])
            inv_rms = per_batch.tile([P, 1], F32, name="inv_rms")
            nc.vector.reciprocal(out=inv_rms[:], in_=rms[:])
            h = per_batch.tile([P, D], BF16, name="h")
            for bank in range(D // N_TILE):
                feats = slice(bank * N_TILE, (bank + 1) * N_TILE)
                nc.vector.scalar_tensor_tensor(
                    out=h[:, feats],
                    in0=x_sb[b][:, feats],
                    scalar=inv_rms[:],
                    in1=gain_all[bank][:],
                    op0=ALU.mult,
                    op1=ALU.mult,
                )
            h_sb.append(h)

        h_grouped = keep.tile([P, BATCH, PASSES, P, PACK], BF16, align_bytes=64)
        h_codes = keep.tile([P, BATCH, PASSES * P], U32, align_bytes=64)
        h_scales = keep.tile([P, BATCH, PASSES * P], U8, align_bytes=64)
        for b in range(BATCH):
            for c in range(PASSES):
                h_t = psum.tile([P, PACK, P], BF16, tag="bank", name="h_t")
                for t in range(PACK):
                    k0 = c * K_PASS + t * P
                    nc.tensor.transpose(
                        out=h_t[:, t, :], in_=h_sb[b][:, k0 : k0 + P], identity=identity[:]
                    )
                nc.scalar.copy(
                    out=h_grouped[:, b, c, :, :], in_=h_t[:].rearrange("p t s -> p s t")
                )
            nc.vector.quantize_mx(
                out=h_codes[:, b, :].bitcast(FP8X4),
                scales=h_scales[:, b, :],
                in_=h_grouped[:, b].rearrange("p c s t -> p (c s t)"),
            )

        w_codes = keep.tile([P, UNITS, PASSES, N_TILE], U32, align_bytes=64)
        w_scales = keep.tile([P, UNITS, PASSES, N_TILE], U8, align_bytes=64)

        def prepare(u):
            j, half = divmod(u, HALVES)
            cols = slice(half * N_TILE, (half + 1) * N_TILE)
            w_grouped = []
            for c in range(PASSES):
                grouped = w_stage.tile([P, N_TILE, PACK], BF16, align_bytes=64, name="grouped")
                by_column = grouped[:].rearrange("p (a i) t -> p a t i", i=RUN)
                by_row = w_raw[(j, c)][:, :, cols].rearrange("p t (a i) -> p a t i", i=RUN)
                nc.vector.tensor_copy(out=by_column[:, :VECTOR_RUNS], in_=by_row[:, :VECTOR_RUNS])
                nc.scalar.copy(out=by_column[:, VECTOR_RUNS:], in_=by_row[:, VECTOR_RUNS:])
                w_grouped.append(grouped)
            for c in range(PASSES):
                nc.vector.quantize_mx(
                    out=w_codes[:, u, c, :].bitcast(FP8X4),
                    scales=w_scales[:, u, c, :],
                    in_=w_grouped[c][:].rearrange("p n t -> p (n t)"),
                )

        def project(u):
            j, half = divmod(u, HALVES)
            cols = slice(half * N_TILE, (half + 1) * N_TILE)
            accs = [psum.tile([P, N_TILE], F32, tag="bank", name="acc") for b in range(BATCH)]
            for c in range(PASSES):
                for b in range(BATCH):
                    nc.tensor.matmul_mx(
                        out=accs[b][:],
                        lhsT=h_codes[:, b, c * P : (c + 1) * P].bitcast(FP8X4),
                        lhsT_scale=h_scales[:, b, c * P : (c + 1) * P],
                        rhs=w_codes[:, u, c, :].bitcast(FP8X4),
                        rhs_scale=w_scales[:, u, c, :],
                        start=(c == 0),
                        stop=(c == PASSES - 1),
                    )
            for b in range(BATCH):
                result = out_stage.tile([P, N_TILE], F32, name="result")
                if u >= UNITS - SHARED_UNITS and b % 2 == 1:
                    nc.vector.tensor_copy(out=result[:], in_=accs[b][:])
                else:
                    nc.scalar.copy(out=result[:], in_=accs[b][:])
                nc.sync.dma_start(out=outs[j][b, :, cols], in_=result[:])

        prepare(0)
        for u in range(UNITS):
            if u + 1 < UNITS:
                prepare(u + 1)
            project(u)
